import numpy as np
import ml_dtypes


def mxq(x, axis, fmt="e4m3"):
    dtype, down = {"e4m3": (ml_dtypes.float8_e4m3fn, 7), "e5m2": (ml_dtypes.float8_e5m2, 14)}[fmt]
    v = np.moveaxis(np.asarray(x, np.float32).astype(ml_dtypes.bfloat16).astype(np.float64), axis, -1)
    blocks = v.reshape(v.shape[:-1] + (-1, 32))
    amax = np.abs(blocks).max(-1, keepdims=True)
    byte = np.maximum(np.where(amax > 0, np.frexp(amax)[1] - 1 + 127, 0) - down, 1)
    scale = np.exp2(byte - 127.0)
    codes = (blocks / scale).astype(np.float32).astype(dtype).astype(np.float64)
    return np.moveaxis((codes * scale).reshape(v.shape), -1, axis)


WIDE = False


def mx_kscale(k):
    if not WIDE:
        return np.ones(k)
    levels = np.array([10, -10, 5, -5, 0])
    a = np.random.permutation(np.resize(levels, k // 512 * 4)).reshape(k // 512, 4)
    idx = np.arange(k)
    return np.exp2(a[idx // 512, idx % 128 // 32])


BF16 = ml_dtypes.bfloat16


def bf(x):
    return np.asarray(x, np.float32).astype(BF16)


def f64(x):
    return np.asarray(x).astype(np.float64)


B, IMG, P0, P1, C, F = 2, 512, 8, 16, 2, 512
E0, E1 = IMG // P0, IMG // P1
N0, N1 = E0 * E0, E1 * E1
D0, D1 = P0 * P0 * C, P1 * P1 * C


def setup_inputs():
    s = mx_kscale(D1)
    flat = np.random.standard_normal((B, N1, D1)) * s
    img = flat.reshape(B, E1, E1, P1, P1, C).transpose(0, 1, 3, 2, 4, 5).reshape(B, IMG, IMG, C)
    encoded = img.reshape(B, E0, P0, E0, P0, C).transpose(0, 1, 3, 2, 4, 5).reshape(B, N0, D0)
    return {"encoded": bf(encoded),
            "W": bf(np.random.standard_normal((D1, F)) / np.sqrt(D1) / s[:, None]),
            "b": bf(np.random.standard_normal(F) * 0.3),
            "pos_emb": bf(np.random.standard_normal((N1, F)) * 0.5)}


def reference(encoded, W, b, pos_emb):
    x = f64(encoded).reshape(-1, E0, E0, P0, P0, C)
    img = x.transpose(0, 1, 3, 2, 4, 5).reshape(-1, IMG, IMG, C)
    new_patches = img.reshape(-1, E1, P1, E1, P1, C).transpose(0, 1, 3, 2, 4, 5)
    flat = new_patches.reshape(-1, N1, D1)
    return (mxq(flat, 2, "e4m3") @ mxq(f64(W), 0, "e4m3")) + f64(b) + f64(pos_emb)

@@ -1,0 +1,148 @@
+from contextlib import ExitStack
+
+import concourse.mybir as mybir
+from concourse.masks import make_identity
+
+F32 = mybir.dt.float32
+BF16 = mybir.dt.bfloat16
+U32 = mybir.dt.uint32
+U8 = mybir.dt.uint8
+FP8X4 = mybir.dt.float8_e4m3fn_x4
+ADD = mybir.AluOpType.add
+
+P = 128
+F = 512
+FLOPS = 2 * 2048 * 512 * 512
+
+POSB_ON_GPSIMD = (0, 2, 4, 5, 6, 7)
+
+
+def tile_resampling_kernel(tc, encoded, W, b, pos_emb, out):
+    nc = tc.nc
+    with ExitStack() as ctx:
+        const = ctx.enter_context(tc.tile_pool(name="const", bufs=1))
+        ps_t = ctx.enter_context(tc.psum_pool(name="ps_t", bufs=3))
+        ps_o = ctx.enter_context(tc.psum_pool(name="ps_o", bufs=4))
+
+        enc_v = encoded.rearrange("i (a q c) d -> i q a (c d)", a=2, q=P, c=16)
+        w_v = W.rearrange("(h s c) f -> s h (c f)", h=2, s=P, c=2)
+        pos_v = pos_emb.rearrange("(m x) f -> m x f", x=8)
+        out_v = out.rearrange("i (m x) f -> i m x f", x=8)
+        chunks = [(0, 0), (1, 0), (0, 1), (1, 1)]
+
+        ident = const.tile([P, P], F32, name="ident")
+        make_identity(nc, ident[:])
+        brow = const.tile([P, F], BF16, name="brow")
+        nc.vector.memset(brow[:], 0.0)
+        ones = const.tile([P, P], BF16, name="ones")
+        nc.vector.memset(ones[:], 1.0)
+
+        nc.sync.dma_start(out=brow[0:1, :], in_=b.rearrange("(o f) -> o f", o=1))
+        w_raw = const.tile([P, 4, F], BF16, name="w_raw")
+        nc.sync.dma_start(out=w_raw[:].rearrange("s (h c) f -> s h (c f)", h=2), in_=w_v)
+        pos = const.tile([P, 8, F], BF16, name="pos")
+        enc_sb = [const.tile([P, 2, 1024], BF16, name="enc%d" % c) for c in range(4)]
+
+        def load_enc(c):
+            i, h = chunks[c]
+            nc.sync.dma_start(out=enc_sb[c][:], in_=enc_v[i][:, :, h * 1024:(h + 1) * 1024])
+
+        nc.sync.dma_start(out=pos[:, 0:4, :], in_=pos_v[:, 0:4, :])
+        load_enc(0)
+        load_enc(1)
+        nc.sync.dma_start(out=pos[:, 4:8, :], in_=pos_v[:, 4:8, :])
+        load_enc(2)
+        load_enc(3)
+
+        perm_tok = const.tile([P, P], F32, name="perm_tok")
+        nc.vector.tensor_copy(
+            out=perm_tok[:].rearrange("q (a x h) -> q a x h", a=16, x=4),
+            in_=ident[:].rearrange("q (a h x) -> q a x h", a=16, h=2),
+        )
+        perm_w = const.tile([P, P], BF16, name="perm_w")
+        nc.vector.tensor_copy(
+            out=perm_w[:].rearrange("s (x y l) -> s x y l", x=2, y=8),
+            in_=ident[:].rearrange("s (y x l) -> s x y l", y=8, x=2),
+        )
+
+        pb = ps_t.tile([P, F], F32, name="pb", tag="t")
+        nc.tensor.matmul(out=pb[:], lhsT=ones[:], rhs=brow[:], start=True, stop=True)
+        bbc = const.tile([P, F], BF16, name="bbc")
+        nc.scalar.copy(out=bbc[:], in_=pb[:])
+
+        w_grp = const.tile([P, F, 4], BF16, name="w_grp", align_bytes=64)
+        for j in range(4):
+            pw = ps_o.tile([P, 4, P], F32, name="pw", tag="o")
+            nc.tensor.matmul(out=pw[:], lhsT=perm_w[:], rhs=w_raw[:, :, j * P:(j + 1) * P],
+                             start=True, stop=True)
+            dst = w_grp[:, j * P:(j + 1) * P, :]
+            src = pw[:].rearrange("p t f -> p f t")
+            if j % 2 == 0:
+                nc.vector.tensor_copy(out=dst, in_=src)
+            else:
+                nc.scalar.copy(out=dst, in_=src)
+        w_codes = const.tile([P, F], U32, name="w_codes", align_bytes=64)
+        w_scales = const.tile([P, F], U8, name="w_scales", align_bytes=64)
+        nc.vector.quantize_mx(out=w_codes[:].bitcast(FP8X4), scales=w_scales[:],
+                              in_=w_grp[:].rearrange("p f t -> p (f t)"))
+
+        posb = const.tile([P, 8, F], F32, name="posb")
+
+        def add_bias(x):
+            eng = nc.gpsimd if x in POSB_ON_GPSIMD else nc.vector
+            eng.tensor_tensor(out=posb[:, x, :], in0=pos[:, x, :], in1=bbc[:], op=ADD)
+
+        grp = [const.tile([P, 2048], BF16, name="grp%d" % c, align_bytes=64) for c in range(4)]
+        codes = [const.tile([P, F], U32, name="codes%d" % c, align_bytes=64) for c in range(4)]
+        scales = [const.tile([P, F], U8, name="scales%d" % c, align_bytes=64) for c in range(4)]
+        res = [const.tile([P, 4, F], F32, name="res%d" % c) for c in range(4)]
+
+        def transposes(c):
+            words = enc_sb[c][:].bitcast(F32)
+            for bank in range(2):
+                pt = ps_t.tile([P, F], F32, name="pt", tag="t")
+                for s in range(4):
+                    xi = bank * 2 + s // 2
+                    a = s % 2
+                    nc.tensor.transpose(pt[:, s * P:(s + 1) * P],
+                                        words[:, a, xi * P:(xi + 1) * P], perm_tok[:])
+                nc.scalar.copy(out=grp[c][:].bitcast(F32)[:, bank * F:(bank + 1) * F], in_=pt[:])
+            for bank in range(2):
+                nc.vector.quantize_mx(
+                    out=codes[c][:, bank * 256:(bank + 1) * 256].bitcast(FP8X4),
+                    scales=scales[c][:, bank * 256:(bank + 1) * 256],
+                    in_=grp[c][:, bank * 1024:(bank + 1) * 1024],
+                )
+
+        def passes(c, cuts):
+            i, h = chunks[c]
+            for xi in range(4):
+                po = ps_o.tile([P, F], F32, name="po", tag="o")
+                nc.tensor.matmul_mx(
+                    out=po[:],
+                    lhsT=codes[c][:, xi * P:(xi + 1) * P].bitcast(FP8X4),
+                    lhsT_scale=scales[c][:, xi * P:(xi + 1) * P],
+                    rhs=w_codes[:].bitcast(FP8X4),
+                    rhs_scale=w_scales[:],
+                    start=True,
+                    stop=True,
+                )
+                nc.vector.tensor_tensor(out=res[c][:, xi, :], in0=po[:], in1=posb[:, h * 4 + xi, :],
+                                        op=ADD)
+                for lo, hi in cuts:
+                    if hi == xi + 1:
+                        nc.sync.dma_start(out=out_v[i][:, h * 4 + lo:h * 4 + hi, :],
+                                          in_=res[c][:, lo:hi, :])
+
+        for x in range(4):
+            add_bias(x)
+        transposes(0)
+        transposes(1)
+        passes(0, [(0, 4)])
+        for x in range(4, 8):
+            add_bias(x)
+        transposes(2)
+        passes(1, [(0, 4)])
+        transposes(3)
+        passes(2, [(0, 4)])
+        passes(3, [(0, 2), (2, 3), (3, 4)])

@@ -14,7 +14,8 @@ P = 128
 F = 512
 FLOPS = 2 * 2048 * 512 * 512
 
-POSB_ON_GPSIMD = (0, 2, 4, 5, 6, 7)
+POSB_ON_GPSIMD = (0, 1, 2, 3, 4, 5, 6, 7)
+CUTS = (((0, 2), (2, 4)), ((0, 2), (2, 4)), ((0, 2), (2, 4)), ((0, 2), (2, 3), (3, 4)))
 
 
 def tile_resampling_kernel(tc, encoded, W, b, pos_emb, out):
@@ -23,6 +24,7 @@ def tile_resampling_kernel(tc, encoded, W, b, pos_emb, out):
         const = ctx.enter_context(tc.tile_pool(name="const", bufs=1))
         ps_t = ctx.enter_context(tc.psum_pool(name="ps_t", bufs=3))
         ps_o = ctx.enter_context(tc.psum_pool(name="ps_o", bufs=4))
+        ctx.enter_context(tc.manual_schedule())
 
         enc_v = encoded.rearrange("i (a q c) d -> i q a (c d)", a=2, q=P, c=16)
         w_v = W.rearrange("(h s c) f -> s h (c f)", h=2, s=P, c=2)
@@ -37,7 +39,7 @@ def tile_resampling_kernel(tc, encoded, W, b, pos_emb, out):
         ones = const.tile([P, P], BF16, name="ones")
         nc.vector.memset(ones[:], 1.0)
 
-        nc.sync.dma_start(out=brow[0:1, :], in_=b.rearrange("(o f) -> o f", o=1))
+        nc.scalar.dma_start(out=brow[0:1, :], in_=b.rearrange("(o f) -> o f", o=1))
         w_raw = const.tile([P, 4, F], BF16, name="w_raw")
         nc.sync.dma_start(out=w_raw[:].rearrange("s (h c) f -> s h (c f)", h=2), in_=w_v)
         pos = const.tile([P, 8, F], BF16, name="pos")
@@ -97,52 +99,67 @@ def tile_resampling_kernel(tc, encoded, W, b, pos_emb, out):
         scales = [const.tile([P, F], U8, name="scales%d" % c, align_bytes=64) for c in range(4)]
         res = [const.tile([P, 4, F], F32, name="res%d" % c) for c in range(4)]
 
-        def transposes(c):
+        def transpose_bank(c, bank):
             words = enc_sb[c][:].bitcast(F32)
-            for bank in range(2):
-                pt = ps_t.tile([P, F], F32, name="pt", tag="t")
-                for s in range(4):
-                    xi = bank * 2 + s // 2
-                    a = s % 2
-                    nc.tensor.transpose(pt[:, s * P:(s + 1) * P],
-                                        words[:, a, xi * P:(xi + 1) * P], perm_tok[:])
-                nc.scalar.copy(out=grp[c][:].bitcast(F32)[:, bank * F:(bank + 1) * F], in_=pt[:])
-            for bank in range(2):
-                nc.vector.quantize_mx(
-                    out=codes[c][:, bank * 256:(bank + 1) * 256].bitcast(FP8X4),
-                    scales=scales[c][:, bank * 256:(bank + 1) * 256],
-                    in_=grp[c][:, bank * 1024:(bank + 1) * 1024],
-                )
+            pt = ps_t.tile([P, F], F32, name="pt", tag="t")
+            for s in range(4):
+                xi = bank * 2 + s // 2
+                a = s % 2
+                nc.tensor.transpose(pt[:, s * P:(s + 1) * P],
+                                    words[:, a, xi * P:(xi + 1) * P], perm_tok[:])
+            return pt
 
-        def passes(c, cuts):
+        def evacuate(c, bank, pt):
+            nc.scalar.copy(out=grp[c][:].bitcast(F32)[:, bank * F:(bank + 1) * F], in_=pt[:])
+
+        def quantise(c, bank):
+            nc.vector.quantize_mx(
+                out=codes[c][:, bank * 256:(bank + 1) * 256].bitcast(FP8X4),
+                scales=scales[c][:, bank * 256:(bank + 1) * 256],
+                in_=grp[c][:, bank * 1024:(bank + 1) * 1024],
+            )
+
+        def transposes(c):
+            banks = [transpose_bank(c, 0), transpose_bank(c, 1)]
+            evacuate(c, 0, banks[0])
+            evacuate(c, 1, banks[1])
+
+        def mx_pass(c, xi):
+            po = ps_o.tile([P, F], F32, name="po", tag="o")
+            nc.tensor.matmul_mx(
+                out=po[:],
+                lhsT=codes[c][:, xi * P:(xi + 1) * P].bitcast(FP8X4),
+                lhsT_scale=scales[c][:, xi * P:(xi + 1) * P],
+                rhs=w_codes[:].bitcast(FP8X4),
+                rhs_scale=w_scales[:],
+                start=True,
+                stop=True,
+            )
+            return po
+
+        def finish(c, xi, po):
+            h = chunks[c][1]
+            nc.vector.tensor_tensor(out=res[c][:, xi, :], in0=po[:], in1=posb[:, h * 4 + xi, :],
+                                    op=ADD)
+
+        def store(c, lo, hi):
             i, h = chunks[c]
-            for xi in range(4):
-                po = ps_o.tile([P, F], F32, name="po", tag="o")
-                nc.tensor.matmul_mx(
-                    out=po[:],
-                    lhsT=codes[c][:, xi * P:(xi + 1) * P].bitcast(FP8X4),
-                    lhsT_scale=scales[c][:, xi * P:(xi + 1) * P],
-                    rhs=w_codes[:].bitcast(FP8X4),
-                    rhs_scale=w_scales[:],
-                    start=True,
-                    stop=True,
-                )
-                nc.vector.tensor_tensor(out=res[c][:, xi, :], in0=po[:], in1=posb[:, h * 4 + xi, :],
-                                        op=ADD)
-                for lo, hi in cuts:
-                    if hi == xi + 1:
-                        nc.sync.dma_start(out=out_v[i][:, h * 4 + lo:h * 4 + hi, :],
-                                          in_=res[c][:, lo:hi, :])
+            nc.sync.dma_start(out=out_v[i][:, h * 4 + lo:h * 4 + hi, :], in_=res[c][:, lo:hi, :])
 
-        for x in range(4):
+        for x in range(8):
             add_bias(x)
         transposes(0)
+        quantise(0, 0)
+        quantise(0, 1)
         transposes(1)
-        passes(0, [(0, 4)])
-        for x in range(4, 8):
-            add_bias(x)
-        transposes(2)
-        passes(1, [(0, 4)])
-        transposes(3)
-        passes(2, [(0, 4)])
-        passes(3, [(0, 2), (2, 3), (3, 4)])
+        for c in range(4):
+            acc = [mx_pass(c, xi) for xi in range(4)]
+            if c + 2 < 4:
+                transposes(c + 2)
+            for xi in range(4):
+                finish(c, xi, acc[xi])
+                if c + 1 < 4 and xi in (1, 2):
+                    quantise(c + 1, xi - 1)
+                for lo, hi in CUTS[c]:
+                    if hi == xi + 1:
+                        store(c, lo, hi)

@@ -14,92 +14,104 @@ P = 128
 F = 512
 FLOPS = 2 * 2048 * 512 * 512
 
-POSB_ON_GPSIMD = (0, 1, 2, 3, 4, 5, 6, 7)
-CUTS = (((0, 2), (2, 4)), ((0, 2), (2, 4)), ((0, 2), (2, 4)), ((0, 2), (2, 3), (3, 4)))
-
 
 def tile_resampling_kernel(tc, encoded, W, b, pos_emb, out):
     nc = tc.nc
     with ExitStack() as ctx:
         const = ctx.enter_context(tc.tile_pool(name="const", bufs=1))
         ps_t = ctx.enter_context(tc.psum_pool(name="ps_t", bufs=3))
-        ps_o = ctx.enter_context(tc.psum_pool(name="ps_o", bufs=4))
+        ps_o = ctx.enter_context(tc.psum_pool(name="ps_o", bufs=5))
         ctx.enter_context(tc.manual_schedule())
 
         enc_v = encoded.rearrange("i (a q c) d -> i q a (c d)", a=2, q=P, c=16)
-        w_v = W.rearrange("(h s c) f -> s h (c f)", h=2, s=P, c=2)
+        w_v = W.rearrange("(h s c) f -> h s (c f)", h=2, s=P, c=2)
         pos_v = pos_emb.rearrange("(m x) f -> m x f", x=8)
         out_v = out.rearrange("i (m x) f -> i m x f", x=8)
         chunks = [(0, 0), (1, 0), (0, 1), (1, 1)]
 
-        ident = const.tile([P, P], F32, name="ident")
-        make_identity(nc, ident[:])
         brow = const.tile([P, F], BF16, name="brow")
         nc.vector.memset(brow[:], 0.0)
         ones = const.tile([P, P], BF16, name="ones")
         nc.vector.memset(ones[:], 1.0)
+        ident = const.tile([P, P], F32, name="ident")
+        make_identity(nc, ident[:])
 
-        nc.scalar.dma_start(out=brow[0:1, :], in_=b.rearrange("(o f) -> o f", o=1))
         w_raw = const.tile([P, 4, F], BF16, name="w_raw")
-        nc.sync.dma_start(out=w_raw[:].rearrange("s (h c) f -> s h (c f)", h=2), in_=w_v)
         pos = const.tile([P, 8, F], BF16, name="pos")
         enc_sb = [const.tile([P, 2, 1024], BF16, name="enc%d" % c) for c in range(4)]
+
+        def load_w(h):
+            nc.sync.dma_start(out=w_raw[:, 2 * h:2 * h + 2, :].rearrange("s c f -> s (c f)"),
+                              in_=w_v[h])
 
         def load_enc(c):
             i, h = chunks[c]
             nc.sync.dma_start(out=enc_sb[c][:], in_=enc_v[i][:, :, h * 1024:(h + 1) * 1024])
 
-        nc.sync.dma_start(out=pos[:, 0:4, :], in_=pos_v[:, 0:4, :])
+        def load_pos(h):
+            nc.sync.dma_start(out=pos[:, 4 * h:4 * h + 4, :], in_=pos_v[:, 4 * h:4 * h + 4, :])
+
+        load_w(0)
+        nc.sync.dma_start(out=brow[0:1, :], in_=b.rearrange("(o f) -> o f", o=1))
+        load_w(1)
+        load_pos(0)
         load_enc(0)
         load_enc(1)
-        nc.sync.dma_start(out=pos[:, 4:8, :], in_=pos_v[:, 4:8, :])
+        load_pos(1)
         load_enc(2)
         load_enc(3)
 
-        perm_tok = const.tile([P, P], F32, name="perm_tok")
-        nc.vector.tensor_copy(
-            out=perm_tok[:].rearrange("q (a x h) -> q a x h", a=16, x=4),
-            in_=ident[:].rearrange("q (a h x) -> q a x h", a=16, h=2),
-        )
         perm_w = const.tile([P, P], BF16, name="perm_w")
         nc.vector.tensor_copy(
             out=perm_w[:].rearrange("s (x y l) -> s x y l", x=2, y=8),
             in_=ident[:].rearrange("s (y x l) -> s x y l", y=8, x=2),
         )
-
-        pb = ps_t.tile([P, F], F32, name="pb", tag="t")
-        nc.tensor.matmul(out=pb[:], lhsT=ones[:], rhs=brow[:], start=True, stop=True)
-        bbc = const.tile([P, F], BF16, name="bbc")
-        nc.scalar.copy(out=bbc[:], in_=pb[:])
+        perm_tok = const.tile([P, P], F32, name="perm_tok")
+        nc.vector.tensor_copy(
+            out=perm_tok[:].rearrange("q (a x h) -> q a x h", a=16, x=4),
+            in_=ident[:].rearrange("q (a h x) -> q a x h", a=16, h=2),
+        )
 
         w_grp = const.tile([P, F, 4], BF16, name="w_grp", align_bytes=64)
+        w_codes = const.tile([P, F], U32, name="w_codes", align_bytes=64)
+        w_scales = const.tile([P, F], U8, name="w_scales", align_bytes=64)
+        bbc = const.tile([P, F], BF16, name="bbc")
+        pw = [ps_o.tile([P, 4, P], F32, name="pw%d" % j, tag="o") for j in range(4)]
+
+        def permute_w(h):
+            for j in range(4):
+                nc.tensor.matmul(out=pw[j][:, 2 * h:2 * h + 2, :], lhsT=perm_w[:],
+                                 rhs=w_raw[:, 2 * h:2 * h + 2, j * P:(j + 1) * P],
+                                 start=True, stop=True)
+
+        permute_w(0)
+        pb = ps_t.tile([P, F], F32, name="pb", tag="t")
+        nc.tensor.matmul(out=pb[:], lhsT=ones[:], rhs=brow[:], start=True, stop=True)
+        nc.scalar.copy(out=bbc[:], in_=pb[:])
+        permute_w(1)
         for j in range(4):
-            pw = ps_o.tile([P, 4, P], F32, name="pw", tag="o")
-            nc.tensor.matmul(out=pw[:], lhsT=perm_w[:], rhs=w_raw[:, :, j * P:(j + 1) * P],
-                             start=True, stop=True)
             dst = w_grp[:, j * P:(j + 1) * P, :]
-            src = pw[:].rearrange("p t f -> p f t")
+            src = pw[j][:].rearrange("p t f -> p f t")
             if j % 2 == 0:
                 nc.vector.tensor_copy(out=dst, in_=src)
             else:
                 nc.scalar.copy(out=dst, in_=src)
-        w_codes = const.tile([P, F], U32, name="w_codes", align_bytes=64)
-        w_scales = const.tile([P, F], U8, name="w_scales", align_bytes=64)
-        nc.vector.quantize_mx(out=w_codes[:].bitcast(FP8X4), scales=w_scales[:],
-                              in_=w_grp[:].rearrange("p f t -> p (f t)"))
+        for k in range(2):
+            nc.vector.quantize_mx(out=w_codes[:, k * 256:(k + 1) * 256].bitcast(FP8X4),
+                                  scales=w_scales[:, k * 256:(k + 1) * 256],
+                                  in_=w_grp[:, k * 256:(k + 1) * 256, :].rearrange("p f t -> p (f t)"))
 
         posb = const.tile([P, 8, F], F32, name="posb")
-
-        def add_bias(x):
-            eng = nc.gpsimd if x in POSB_ON_GPSIMD else nc.vector
-            eng.tensor_tensor(out=posb[:, x, :], in0=pos[:, x, :], in1=bbc[:], op=ADD)
+        for x in range(8):
+            nc.gpsimd.tensor_tensor(out=posb[:, x, :], in0=pos[:, x, :], in1=bbc[:], op=ADD)
 
         grp = [const.tile([P, 2048], BF16, name="grp%d" % c, align_bytes=64) for c in range(4)]
         codes = [const.tile([P, F], U32, name="codes%d" % c, align_bytes=64) for c in range(4)]
         scales = [const.tile([P, F], U8, name="scales%d" % c, align_bytes=64) for c in range(4)]
         res = [const.tile([P, 4, F], F32, name="res%d" % c) for c in range(4)]
 
-        def transpose_bank(c, bank):
+        def transpose_unit(u):
+            c, bank = u // 2, u % 2
             words = enc_sb[c][:].bitcast(F32)
             pt = ps_t.tile([P, F], F32, name="pt", tag="t")
             for s in range(4):
@@ -109,22 +121,25 @@ def tile_resampling_kernel(tc, encoded, W, b, pos_emb, out):
                                     words[:, a, xi * P:(xi + 1) * P], perm_tok[:])
             return pt
 
-        def evacuate(c, bank, pt):
+        def evacuate(u, pt):
+            c, bank = u // 2, u % 2
             nc.scalar.copy(out=grp[c][:].bitcast(F32)[:, bank * F:(bank + 1) * F], in_=pt[:])
 
-        def quantise(c, bank):
+        def transpose_pair(u):
+            banks = [transpose_unit(u), transpose_unit(u + 1)]
+            evacuate(u, banks[0])
+            evacuate(u + 1, banks[1])
+
+        def quantise(u):
+            c, bank = u // 2, u % 2
             nc.vector.quantize_mx(
                 out=codes[c][:, bank * 256:(bank + 1) * 256].bitcast(FP8X4),
                 scales=scales[c][:, bank * 256:(bank + 1) * 256],
                 in_=grp[c][:, bank * 1024:(bank + 1) * 1024],
             )
 
-        def transposes(c):
-            banks = [transpose_bank(c, 0), transpose_bank(c, 1)]
-            evacuate(c, 0, banks[0])
-            evacuate(c, 1, banks[1])
-
-        def mx_pass(c, xi):
+        def mx_pass(n):
+            c, xi = n // 4, n % 4
             po = ps_o.tile([P, F], F32, name="po", tag="o")
             nc.tensor.matmul_mx(
                 out=po[:],
@@ -137,29 +152,31 @@ def tile_resampling_kernel(tc, encoded, W, b, pos_emb, out):
             )
             return po
 
-        def finish(c, xi, po):
+        def finish(n, po):
+            c, xi = n // 4, n % 4
             h = chunks[c][1]
             nc.vector.tensor_tensor(out=res[c][:, xi, :], in0=po[:], in1=posb[:, h * 4 + xi, :],
                                     op=ADD)
 
-        def store(c, lo, hi):
+        def store(n_lo, n_hi):
+            c, lo, hi = n_lo // 4, n_lo % 4, n_hi - (n_lo // 4) * 4
             i, h = chunks[c]
             nc.sync.dma_start(out=out_v[i][:, h * 4 + lo:h * 4 + hi, :], in_=res[c][:, lo:hi, :])
 
-        for x in range(8):
-            add_bias(x)
-        transposes(0)
-        quantise(0, 0)
-        quantise(0, 1)
-        transposes(1)
-        for c in range(4):
-            acc = [mx_pass(c, xi) for xi in range(4)]
-            if c + 2 < 4:
-                transposes(c + 2)
-            for xi in range(4):
-                finish(c, xi, acc[xi])
-                if c + 1 < 4 and xi in (1, 2):
-                    quantise(c + 1, xi - 1)
-                for lo, hi in CUTS[c]:
-                    if hi == xi + 1:
-                        store(c, lo, hi)
+        transpose_pair(0)
+        quantise(0)
+        quantise(1)
+        transpose_pair(2)
+        for g in range(4):
+            acc = [mx_pass(4 * g + k) for k in range(4)]
+            if g < 2:
+                transpose_pair(2 * g + 4)
+            for u in (2 * g, 2 * g + 1):
+                if u + 2 < 8:
+                    quantise(u + 2)
+                for n in (2 * u, 2 * u + 1):
+                    finish(n, acc[n - 4 * g])
+                    if u == 7:
+                        store(n, n + 1)
+                if u < 7:
+                    store(2 * u, 2 * u + 2)

@@ -5,6 +5,7 @@ from concourse.masks import make_identity
 
 F32 = mybir.dt.float32
 BF16 = mybir.dt.bfloat16
+I32 = mybir.dt.int32
 U32 = mybir.dt.uint32
 U8 = mybir.dt.uint8
 FP8X4 = mybir.dt.float8_e4m3fn_x4
@@ -20,7 +21,7 @@ def tile_resampling_kernel(tc, encoded, W, b, pos_emb, out):
     with ExitStack() as ctx:
         const = ctx.enter_context(tc.tile_pool(name="const", bufs=1))
         ps_t = ctx.enter_context(tc.psum_pool(name="ps_t", bufs=3))
-        ps_o = ctx.enter_context(tc.psum_pool(name="ps_o", bufs=5))
+        ps_o = ctx.enter_context(tc.psum_pool(name="ps_o", bufs=4))
         ctx.enter_context(tc.manual_schedule())
 
         enc_v = encoded.rearrange("i (a q c) d -> i q a (c d)", a=2, q=P, c=16)
@@ -54,8 +55,8 @@ def tile_resampling_kernel(tc, encoded, W, b, pos_emb, out):
         load_w(0)
         nc.sync.dma_start(out=brow[0:1, :], in_=b.rearrange("(o f) -> o f", o=1))
         load_w(1)
-        load_pos(0)
         load_enc(0)
+        load_pos(0)
         load_enc(1)
         load_pos(1)
         load_enc(2)
@@ -78,17 +79,22 @@ def tile_resampling_kernel(tc, encoded, W, b, pos_emb, out):
         bbc = const.tile([P, F], BF16, name="bbc")
         pw = [ps_o.tile([P, 4, P], F32, name="pw%d" % j, tag="o") for j in range(4)]
 
-        def permute_w(h):
-            for j in range(4):
-                nc.tensor.matmul(out=pw[j][:, 2 * h:2 * h + 2, :], lhsT=perm_w[:],
-                                 rhs=w_raw[:, 2 * h:2 * h + 2, j * P:(j + 1) * P],
-                                 start=True, stop=True)
+        def permute_w(h, j):
+            nc.tensor.matmul(out=pw[j][:, 2 * h:2 * h + 2, :], lhsT=perm_w[:],
+                             rhs=w_raw[:, 2 * h:2 * h + 2, j * P:(j + 1) * P],
+                             start=True, stop=True)
 
-        permute_w(0)
+        permute_w(0, 0)
         pb = ps_t.tile([P, F], F32, name="pb", tag="t")
         nc.tensor.matmul(out=pb[:], lhsT=ones[:], rhs=brow[:], start=True, stop=True)
         nc.scalar.copy(out=bbc[:], in_=pb[:])
-        permute_w(1)
+        permute_w(0, 1)
+        permute_w(1, 0)
+        permute_w(1, 1)
+        permute_w(0, 2)
+        permute_w(0, 3)
+        permute_w(1, 2)
+        permute_w(1, 3)
         for j in range(4):
             dst = w_grp[:, j * P:(j + 1) * P, :]
             src = pw[j][:].rearrange("p t f -> p f t")
@@ -102,8 +108,12 @@ def tile_resampling_kernel(tc, encoded, W, b, pos_emb, out):
                                   in_=w_grp[:, k * 256:(k + 1) * 256, :].rearrange("p f t -> p (f t)"))
 
         posb = const.tile([P, 8, F], F32, name="posb")
-        for x in range(8):
-            nc.gpsimd.tensor_tensor(out=posb[:, x, :], in0=pos[:, x, :], in1=bbc[:], op=ADD)
+
+        def add_bias(eng, x):
+            eng.tensor_tensor(out=posb[:, x, :], in0=pos[:, x, :], in1=bbc[:], op=ADD)
+
+        for x in range(1, 8):
+            add_bias(nc.gpsimd, x)
 
         grp = [const.tile([P, 2048], BF16, name="grp%d" % c, align_bytes=64) for c in range(4)]
         codes = [const.tile([P, F], U32, name="codes%d" % c, align_bytes=64) for c in range(4)]
@@ -154,29 +164,29 @@ def tile_resampling_kernel(tc, encoded, W, b, pos_emb, out):
 
         def finish(n, po):
             c, xi = n // 4, n % 4
-            h = chunks[c][1]
+            i, h = chunks[c]
             nc.vector.tensor_tensor(out=res[c][:, xi, :], in0=po[:], in1=posb[:, h * 4 + xi, :],
                                     op=ADD)
+            nc.sync.dma_start(out=out_v[i][:, h * 4 + xi, :], in_=res[c][:, xi, :])
 
-        def store(n_lo, n_hi):
-            c, lo, hi = n_lo // 4, n_lo % 4, n_hi - (n_lo // 4) * 4
-            i, h = chunks[c]
-            nc.sync.dma_start(out=out_v[i][:, h * 4 + lo:h * 4 + hi, :], in_=res[c][:, lo:hi, :])
+        def finish_unit(u, acc):
+            finish(2 * u, acc[0])
+            finish(2 * u + 1, acc[1])
+            if u + 2 < 8:
+                quantise(u + 2)
 
         transpose_pair(0)
         quantise(0)
+        add_bias(nc.vector, 0)
         quantise(1)
+        first = [mx_pass(0), mx_pass(1)]
         transpose_pair(2)
-        for g in range(4):
+        second = [mx_pass(2), mx_pass(3)]
+        finish_unit(0, first)
+        finish_unit(1, second)
+        for g in range(1, 4):
+            if g < 3:
+                transpose_pair(2 * g + 2)
             acc = [mx_pass(4 * g + k) for k in range(4)]
-            if g < 2:
-                transpose_pair(2 * g + 4)
-            for u in (2 * g, 2 * g + 1):
-                if u + 2 < 8:
-                    quantise(u + 2)
-                for n in (2 * u, 2 * u + 1):
-                    finish(n, acc[n - 4 * g])
-                    if u == 7:
-                        store(n, n + 1)
-                if u < 7:
-                    store(2 * u, 2 * u + 2)
+            finish_unit(2 * g, acc[0:2])
+            finish_unit(2 * g + 1, acc[2:4])

@@ -5,7 +5,6 @@ from concourse.masks import make_identity
 
 F32 = mybir.dt.float32
 BF16 = mybir.dt.bfloat16
-I32 = mybir.dt.int32
 U32 = mybir.dt.uint32
 U8 = mybir.dt.uint8
 FP8X4 = mybir.dt.float8_e4m3fn_x4
@@ -22,6 +21,7 @@ def tile_resampling_kernel(tc, encoded, W, b, pos_emb, out):
         const = ctx.enter_context(tc.tile_pool(name="const", bufs=1))
         ps_t = ctx.enter_context(tc.psum_pool(name="ps_t", bufs=3))
         ps_o = ctx.enter_context(tc.psum_pool(name="ps_o", bufs=4))
+        ps_w = ctx.enter_context(tc.psum_pool(name="ps_w", bufs=1))
         ctx.enter_context(tc.manual_schedule())
 
         enc_v = encoded.rearrange("i (a q c) d -> i q a (c d)", a=2, q=P, c=16)
@@ -32,10 +32,25 @@ def tile_resampling_kernel(tc, encoded, W, b, pos_emb, out):
 
         brow = const.tile([P, F], BF16, name="brow")
         nc.vector.memset(brow[:], 0.0)
+        z_vals = const.tile([P, F], BF16, name="z_vals", align_bytes=64)
+        nc.vector.memset(z_vals[:], 0.0)
+        z_codes = const.tile([P, P], U32, name="z_codes", align_bytes=64)
+        z_scales = const.tile([P, P], U8, name="z_scales", align_bytes=64)
+        nc.vector.quantize_mx(out=z_codes[:].bitcast(FP8X4), scales=z_scales[:], in_=z_vals[:])
         ones = const.tile([P, P], BF16, name="ones")
         nc.vector.memset(ones[:], 1.0)
         ident = const.tile([P, P], F32, name="ident")
         make_identity(nc, ident[:])
+
+        idle = ps_w.tile([P, P], F32, name="idle")
+
+        def keep_warm(count):
+            for k in range(count):
+                nc.tensor.matmul_mx(out=idle[:], lhsT=z_codes[:].bitcast(FP8X4),
+                                    lhsT_scale=z_scales[:], rhs=z_codes[:].bitcast(FP8X4),
+                                    rhs_scale=z_scales[:], start=True, stop=True)
+
+        keep_warm(12)
 
         w_raw = const.tile([P, 4, F], BF16, name="w_raw")
         pos = const.tile([P, 8, F], BF16, name="pos")
@@ -176,6 +191,7 @@ def tile_resampling_kernel(tc, encoded, W, b, pos_emb, out):
                 quantise(u + 2)
 
         transpose_pair(0)
+        keep_warm(12)
         quantise(0)
         add_bias(nc.vector, 0)
         quantise(1)

@@ -21,7 +21,6 @@ def tile_resampling_kernel(tc, encoded, W, b, pos_emb, out):
         const = ctx.enter_context(tc.tile_pool(name="const", bufs=1))
         ps_t = ctx.enter_context(tc.psum_pool(name="ps_t", bufs=3))
         ps_o = ctx.enter_context(tc.psum_pool(name="ps_o", bufs=4))
-        ps_w = ctx.enter_context(tc.psum_pool(name="ps_w", bufs=1))
         ctx.enter_context(tc.manual_schedule())
 
         enc_v = encoded.rearrange("i (a q c) d -> i q a (c d)", a=2, q=P, c=16)
@@ -32,25 +31,10 @@ def tile_resampling_kernel(tc, encoded, W, b, pos_emb, out):
 
         brow = const.tile([P, F], BF16, name="brow")
         nc.vector.memset(brow[:], 0.0)
-        z_vals = const.tile([P, F], BF16, name="z_vals", align_bytes=64)
-        nc.vector.memset(z_vals[:], 0.0)
-        z_codes = const.tile([P, P], U32, name="z_codes", align_bytes=64)
-        z_scales = const.tile([P, P], U8, name="z_scales", align_bytes=64)
-        nc.vector.quantize_mx(out=z_codes[:].bitcast(FP8X4), scales=z_scales[:], in_=z_vals[:])
         ones = const.tile([P, P], BF16, name="ones")
         nc.vector.memset(ones[:], 1.0)
         ident = const.tile([P, P], F32, name="ident")
         make_identity(nc, ident[:])
-
-        idle = ps_w.tile([P, P], F32, name="idle")
-
-        def keep_warm(count):
-            for k in range(count):
-                nc.tensor.matmul_mx(out=idle[:], lhsT=z_codes[:].bitcast(FP8X4),
-                                    lhsT_scale=z_scales[:], rhs=z_codes[:].bitcast(FP8X4),
-                                    rhs_scale=z_scales[:], start=True, stop=True)
-
-        keep_warm(12)
 
         w_raw = const.tile([P, 4, F], BF16, name="w_raw")
         pos = const.tile([P, 8, F], BF16, name="pos")
@@ -99,36 +83,39 @@ def tile_resampling_kernel(tc, encoded, W, b, pos_emb, out):
                              rhs=w_raw[:, 2 * h:2 * h + 2, j * P:(j + 1) * P],
                              start=True, stop=True)
 
-        permute_w(0, 0)
-        pb = ps_t.tile([P, F], F32, name="pb", tag="t")
-        nc.tensor.matmul(out=pb[:], lhsT=ones[:], rhs=brow[:], start=True, stop=True)
-        nc.scalar.copy(out=bbc[:], in_=pb[:])
-        permute_w(0, 1)
-        permute_w(1, 0)
-        permute_w(1, 1)
-        permute_w(0, 2)
-        permute_w(0, 3)
-        permute_w(1, 2)
-        permute_w(1, 3)
-        for j in range(4):
-            dst = w_grp[:, j * P:(j + 1) * P, :]
-            src = pw[j][:].rearrange("p t f -> p f t")
-            if j % 2 == 0:
-                nc.vector.tensor_copy(out=dst, in_=src)
-            else:
-                nc.scalar.copy(out=dst, in_=src)
-        for k in range(2):
-            nc.vector.quantize_mx(out=w_codes[:, k * 256:(k + 1) * 256].bitcast(FP8X4),
-                                  scales=w_scales[:, k * 256:(k + 1) * 256],
-                                  in_=w_grp[:, k * 256:(k + 1) * 256, :].rearrange("p f t -> p (f t)"))
-
         posb = const.tile([P, 8, F], F32, name="posb")
 
         def add_bias(eng, x):
             eng.tensor_tensor(out=posb[:, x, :], in0=pos[:, x, :], in1=bbc[:], op=ADD)
 
-        for x in range(1, 8):
-            add_bias(nc.gpsimd, x)
+        def regroup_w(eng_copy, j):
+            eng_copy(out=w_grp[:, j * P:(j + 1) * P, :], in_=pw[j][:].rearrange("p t f -> p f t"))
+
+        def quantise_w(k):
+            nc.vector.quantize_mx(out=w_codes[:, k * 256:(k + 1) * 256].bitcast(FP8X4),
+                                  scales=w_scales[:, k * 256:(k + 1) * 256],
+                                  in_=w_grp[:, k * 256:(k + 1) * 256, :].rearrange("p f t -> p (f t)"))
+
+        permute_w(0, 0)
+        permute_w(0, 1)
+        permute_w(1, 0)
+        permute_w(1, 1)
+        permute_w(0, 2)
+        permute_w(1, 2)
+        pb = ps_t.tile([P, F], F32, name="pb", tag="t")
+        nc.tensor.matmul(out=pb[:], lhsT=ones[:], rhs=brow[:], start=True, stop=True)
+        permute_w(0, 3)
+        permute_w(1, 3)
+        regroup_w(nc.vector.tensor_copy, 0)
+        regroup_w(nc.scalar.copy, 1)
+        regroup_w(nc.vector.tensor_copy, 2)
+        nc.scalar.copy(out=bbc[:], in_=pb[:])
+        regroup_w(nc.scalar.copy, 3)
+        quantise_w(0)
+        add_bias(nc.gpsimd, 0)
+        add_bias(nc.gpsimd, 1)
+        add_bias(nc.vector, 3)
+        quantise_w(1)
 
         grp = [const.tile([P, 2048], BF16, name="grp%d" % c, align_bytes=64) for c in range(4)]
         codes = [const.tile([P, F], U32, name="codes%d" % c, align_bytes=64) for c in range(4)]
@@ -184,25 +171,19 @@ def tile_resampling_kernel(tc, encoded, W, b, pos_emb, out):
                                     op=ADD)
             nc.sync.dma_start(out=out_v[i][:, h * 4 + xi, :], in_=res[c][:, xi, :])
 
-        def finish_unit(u, acc):
-            finish(2 * u, acc[0])
-            finish(2 * u + 1, acc[1])
-            if u + 2 < 8:
-                quantise(u + 2)
-
         transpose_pair(0)
-        keep_warm(12)
         quantise(0)
-        add_bias(nc.vector, 0)
+        add_bias(nc.vector, 2)
         quantise(1)
-        first = [mx_pass(0), mx_pass(1)]
         transpose_pair(2)
-        second = [mx_pass(2), mx_pass(3)]
-        finish_unit(0, first)
-        finish_unit(1, second)
-        for g in range(1, 4):
-            if g < 3:
-                transpose_pair(2 * g + 2)
+        for x in range(4, 8):
+            add_bias(nc.gpsimd, x)
+        for g in range(4):
             acc = [mx_pass(4 * g + k) for k in range(4)]
-            finish_unit(2 * g, acc[0:2])
-            finish_unit(2 * g + 1, acc[2:4])
+            if g < 2:
+                transpose_pair(2 * g + 4)
+            for u in (2 * g, 2 * g + 1):
+                if u + 2 < 8:
+                    quantise(u + 2)
+                finish(2 * u, acc[2 * u - 4 * g])
+                finish(2 * u + 1, acc[2 * u + 1 - 4 * g])

from contextlib import ExitStack

import concourse.mybir as mybir
from concourse.masks import make_identity

F32 = mybir.dt.float32
BF16 = mybir.dt.bfloat16
U32 = mybir.dt.uint32
U8 = mybir.dt.uint8
FP8X4 = mybir.dt.float8_e4m3fn_x4
ADD = mybir.AluOpType.add

P = 128
F = 512
FLOPS = 2 * 2048 * 512 * 512


def tile_resampling_kernel(tc, encoded, W, b, pos_emb, out):
    nc = tc.nc
    with ExitStack() as ctx:
        const = ctx.enter_context(tc.tile_pool(name="const", bufs=1))
        ps_t = ctx.enter_context(tc.psum_pool(name="ps_t", bufs=3))
        ps_o = ctx.enter_context(tc.psum_pool(name="ps_o", bufs=4))
        ctx.enter_context(tc.manual_schedule())

        enc_v = encoded.rearrange("i (a q c) d -> i q a (c d)", a=2, q=P, c=16)
        w_v = W.rearrange("(h s c) f -> h s (c f)", h=2, s=P, c=2)
        pos_v = pos_emb.rearrange("(m x) f -> m x f", x=8)
        out_v = out.rearrange("i (m x) f -> i m x f", x=8)
        chunks = [(0, 0), (1, 0), (0, 1), (1, 1)]

        brow = const.tile([P, F], BF16, name="brow")
        nc.vector.memset(brow[:], 0.0)
        ones = const.tile([P, P], BF16, name="ones")
        nc.vector.memset(ones[:], 1.0)
        ident = const.tile([P, P], F32, name="ident")
        make_identity(nc, ident[:])

        w_raw = const.tile([P, 4, F], BF16, name="w_raw")
        pos = const.tile([P, 8, F], BF16, name="pos")
        enc_sb = [const.tile([P, 2, 1024], BF16, name="enc%d" % c) for c in range(4)]

        def load_w(h):
            nc.sync.dma_start(out=w_raw[:, 2 * h:2 * h + 2, :].rearrange("s c f -> s (c f)"),
                              in_=w_v[h])

        def load_enc(c):
            i, h = chunks[c]
            nc.sync.dma_start(out=enc_sb[c][:], in_=enc_v[i][:, :, h * 1024:(h + 1) * 1024])

        def load_pos(h):
            nc.sync.dma_start(out=pos[:, 4 * h:4 * h + 4, :], in_=pos_v[:, 4 * h:4 * h + 4, :])

        load_w(0)
        nc.sync.dma_start(out=brow[0:1, :], in_=b.rearrange("(o f) -> o f", o=1))
        load_w(1)
        load_enc(0)
        load_pos(0)
        load_enc(1)
        load_pos(1)
        load_enc(2)
        load_enc(3)

        perm_w = const.tile([P, P], BF16, name="perm_w")
        nc.vector.tensor_copy(
            out=perm_w[:].rearrange("s (x y l) -> s x y l", x=2, y=8),
            in_=ident[:].rearrange("s (y x l) -> s x y l", y=8, x=2),
        )
        perm_tok = const.tile([P, P], F32, name="perm_tok")
        nc.vector.tensor_copy(
            out=perm_tok[:].rearrange("q (a x h) -> q a x h", a=16, x=4),
            in_=ident[:].rearrange("q (a h x) -> q a x h", a=16, h=2),
        )

        w_grp = const.tile([P, F, 4], BF16, name="w_grp", align_bytes=64)
        w_codes = const.tile([P, F], U32, name="w_codes", align_bytes=64)
        w_scales = const.tile([P, F], U8, name="w_scales", align_bytes=64)
        bbc = const.tile([P, F], BF16, name="bbc")
        pw = [ps_o.tile([P, 4, P], F32, name="pw%d" % j, tag="o") for j in range(4)]

        def permute_w(h, j):
            nc.tensor.matmul(out=pw[j][:, 2 * h:2 * h + 2, :], lhsT=perm_w[:],
                             rhs=w_raw[:, 2 * h:2 * h + 2, j * P:(j + 1) * P],
                             start=True, stop=True)

        posb = const.tile([P, 8, F], F32, name="posb")

        def add_bias(eng, x):
            eng.tensor_tensor(out=posb[:, x, :], in0=pos[:, x, :], in1=bbc[:], op=ADD)

        def regroup_w(eng_copy, j):
            eng_copy(out=w_grp[:, j * P:(j + 1) * P, :], in_=pw[j][:].rearrange("p t f -> p f t"))

        def quantise_w(k):
            nc.vector.quantize_mx(out=w_codes[:, k * 256:(k + 1) * 256].bitcast(FP8X4),
                                  scales=w_scales[:, k * 256:(k + 1) * 256],
                                  in_=w_grp[:, k * 256:(k + 1) * 256, :].rearrange("p f t -> p (f t)"))

        permute_w(0, 0)
        permute_w(0, 1)
        permute_w(1, 0)
        permute_w(1, 1)
        permute_w(0, 2)
        permute_w(1, 2)
        pb = ps_t.tile([P, F], F32, name="pb", tag="t")
        nc.tensor.matmul(out=pb[:], lhsT=ones[:], rhs=brow[:], start=True, stop=True)
        permute_w(0, 3)
        permute_w(1, 3)
        regroup_w(nc.vector.tensor_copy, 0)
        regroup_w(nc.scalar.copy, 1)
        regroup_w(nc.vector.tensor_copy, 2)
        nc.scalar.copy(out=bbc[:], in_=pb[:])
        regroup_w(nc.scalar.copy, 3)
        quantise_w(0)
        add_bias(nc.gpsimd, 0)
        add_bias(nc.gpsimd, 1)
        add_bias(nc.vector, 3)
        quantise_w(1)

        grp = [const.tile([P, 2048], BF16, name="grp%d" % c, align_bytes=64) for c in range(4)]
        codes = [const.tile([P, F], U32, name="codes%d" % c, align_bytes=64) for c in range(4)]
        scales = [const.tile([P, F], U8, name="scales%d" % c, align_bytes=64) for c in range(4)]
        res = [const.tile([P, 4, F], F32, name="res%d" % c) for c in range(4)]

        def transpose_unit(u):
            c, bank = u // 2, u % 2
            words = enc_sb[c][:].bitcast(F32)
            pt = ps_t.tile([P, F], F32, name="pt", tag="t")
            for s in range(4):
                xi = bank * 2 + s // 2
                a = s % 2
                nc.tensor.transpose(pt[:, s * P:(s + 1) * P],
                                    words[:, a, xi * P:(xi + 1) * P], perm_tok[:])
            return pt

        def evacuate(u, pt):
            c, bank = u // 2, u % 2
            nc.scalar.copy(out=grp[c][:].bitcast(F32)[:, bank * F:(bank + 1) * F], in_=pt[:])

        def transpose_pair(u):
            banks = [transpose_unit(u), transpose_unit(u + 1)]
            evacuate(u, banks[0])
            evacuate(u + 1, banks[1])

        def quantise(u):
            c, bank = u // 2, u % 2
            nc.vector.quantize_mx(
                out=codes[c][:, bank * 256:(bank + 1) * 256].bitcast(FP8X4),
                scales=scales[c][:, bank * 256:(bank + 1) * 256],
                in_=grp[c][:, bank * 1024:(bank + 1) * 1024],
            )

        def mx_pass(n):
            c, xi = n // 4, n % 4
            po = ps_o.tile([P, F], F32, name="po", tag="o")
            nc.tensor.matmul_mx(
                out=po[:],
                lhsT=codes[c][:, xi * P:(xi + 1) * P].bitcast(FP8X4),
                lhsT_scale=scales[c][:, xi * P:(xi + 1) * P],
                rhs=w_codes[:].bitcast(FP8X4),
                rhs_scale=w_scales[:],
                start=True,
                stop=True,
            )
            return po

        def finish(n, po):
            c, xi = n // 4, n % 4
            i, h = chunks[c]
            nc.vector.tensor_tensor(out=res[c][:, xi, :], in0=po[:], in1=posb[:, h * 4 + xi, :],
                                    op=ADD)
            nc.sync.dma_start(out=out_v[i][:, h * 4 + xi, :], in_=res[c][:, xi, :])

        transpose_pair(0)
        quantise(0)
        add_bias(nc.vector, 2)
        quantise(1)
        transpose_pair(2)
        for x in range(4, 8):
            add_bias(nc.gpsimd, x)
        for g in range(4):
            acc = [mx_pass(4 * g + k) for k in range(4)]
            if g < 2:
                transpose_pair(2 * g + 4)
            for u in (2 * g, 2 * g + 1):
                if u + 2 < 8:
                    quantise(u + 2)
                finish(2 * u, acc[2 * u - 4 * g])
                finish(2 * u + 1, acc[2 * u + 1 - 4 * g])
